import numpy as np
import ml_dtypes


def mxq(x, axis, fmt="e4m3"):
    dtype, down = {"e4m3": (ml_dtypes.float8_e4m3fn, 7), "e5m2": (ml_dtypes.float8_e5m2, 14)}[fmt]
    v = np.moveaxis(np.asarray(x, np.float32).astype(ml_dtypes.bfloat16).astype(np.float64), axis, -1)
    blocks = v.reshape(v.shape[:-1] + (-1, 32))
    amax = np.abs(blocks).max(-1, keepdims=True)
    byte = np.maximum(np.where(amax > 0, np.frexp(amax)[1] - 1 + 127, 0) - down, 1)
    scale = np.exp2(byte - 127.0)
    codes = (blocks / scale).astype(np.float32).astype(dtype).astype(np.float64)
    return np.moveaxis((codes * scale).reshape(v.shape), -1, axis)


WIDE = False


def mx_kscale(k):
    if not WIDE:
        return np.ones(k)
    levels = np.array([10, -10, 5, -5, 0])
    if k % 512:
        return np.exp2(np.random.permutation(np.resize(levels, k // 32))).repeat(32)
    a = np.empty((k // 512, 16))
    for p in range(k // 512):
        a[p, :8] = np.random.permutation(np.resize(levels, 8))
        for g in range(8):
            far = levels[np.abs(levels - a[p, g]) >= 10]
            a[p, g + 8] = far[np.random.randint(len(far))]
    return np.exp2(a.ravel()).repeat(32)


BF16 = ml_dtypes.bfloat16


def bf(x):
    return np.asarray(x, np.float32).astype(BF16)


def f64(x):
    return np.asarray(x).astype(np.float64)


NS, NI, T = 384, 128, 8193
NA = NS + NI


def setup_inputs():
    s = mx_kscale(NA)
    r = s[:NS]
    A = np.random.standard_normal((NS, NS)) / np.sqrt(NA)
    B = np.random.standard_normal((NS, NI)) / np.sqrt(NA)
    x0 = np.random.standard_normal(NS) * 3.0
    V = np.random.standard_normal((T, NA))
    V[0, :NS] *= 3.0
    return {"A": bf(A * r[:, None] / s[None, :NS]), "B": bf(B * r[:, None] / s[None, NS:]), "x0": bf(x0 * r),
            "net_input": bf((V * s[None, :]).reshape(-1)), "T": T}


def reference(A, B, x0, net_input, T):
    n_state = A.shape[0]
    n_all = n_state + B.shape[1]
    AB = np.concatenate([f64(A), f64(B)], axis=1)
    V = f64(net_input).reshape(T, n_all)
    out0 = V[0, :n_state] - f64(x0)
    prop = mxq(V[:-1], 1, "e4m3") @ mxq(AB, 1, "e4m3").T
    out_rest = prop - V[1:, :n_state]
    return np.concatenate([out0, out_rest.reshape(-1)])

@@ -1,0 +1,173 @@
+from contextlib import ExitStack
+
+import concourse.mybir as mybir
+from concourse.masks import make_identity
+
+F32 = mybir.dt.float32
+BF16 = mybir.dt.bfloat16
+U32 = mybir.dt.uint32
+U8 = mybir.dt.uint8
+FP8X4 = mybir.dt.float8_e4m3fn_x4
+SUB = mybir.AluOpType.subtract
+
+P = 128
+NS = 384
+NA = 512
+STEPS = 8192
+J = STEPS // P
+GROUP = 4
+LOAD_CHUNKS = [4, 4, 8, 16, 32]
+STORE_CHUNKS = [8, 8, 8, 8, 8, 8, 8, 4, 2, 2]
+OFFLOAD = 0
+FLOPS = 2 * STEPS * NS * NA
+
+
+def tile_constrainnet_t_kernel(tc, A, B, x0, net_input, T, out):
+    nc = tc.nc
+    assert T == STEPS + 1
+    n_groups = J // GROUP
+    with ExitStack() as ctx:
+        const = ctx.enter_context(tc.tile_pool(name="const", bufs=1))
+        vpool = ctx.enter_context(tc.tile_pool(name="vpool", bufs=1))
+        opool = ctx.enter_context(tc.tile_pool(name="opool", bufs=1))
+        gpool = ctx.enter_context(tc.tile_pool(name="gpool", bufs=3))
+        qpool = ctx.enter_context(tc.tile_pool(name="qpool", bufs=3))
+        xt_ps = ctx.enter_context(tc.psum_pool(name="xt_ps", bufs=3))
+        pr_ps = ctx.enter_context(tc.psum_pool(name="pr_ps", bufs=5))
+
+        ctx.enter_context(tc.manual_schedule())
+
+        ident = const.tile([P, P], F32, name="ident")
+        make_identity(nc, ident[:])
+
+        x0_sb = const.tile([1, NS], BF16, name="x0_sb")
+        nc.sync.dma_start(out=x0_sb[:], in_=x0.rearrange("(o n) -> o n", o=1))
+        ab_sb = const.tile([P, 3, NA], BF16, name="ab_sb")
+        nc.sync.dma_start(out=ab_sb[:, :, 0:NS], in_=A.rearrange("(r p) k -> p r k", p=P))
+        nc.sync.dma_start(out=ab_sb[:, :, NS:NA], in_=B.rearrange("(r p) k -> p r k", p=P))
+        v_rows = net_input[0 : STEPS * NA].rearrange("(p j k) -> p j k", p=P, j=J)
+        where = []
+        j0 = 0
+        for c, n in enumerate(LOAD_CHUNKS):
+            vt = vpool.tile([P, n, NA], BF16, name="v%d" % c)
+            nc.sync.dma_start(out=vt[:], in_=v_rows[:, j0 : j0 + n, :])
+            for i in range(n):
+                where.append((vt, i))
+            j0 += n
+        assert j0 == J
+        v_next = net_input[NA : (STEPS + 1) * NA].rearrange("(p j k) -> p j k", p=P, j=J)
+        v_last = vpool.tile([P, 1, NS], BF16, name="v_last")
+        nc.sync.dma_start(out=v_last[:], in_=v_next[:, J - 1 : J, 0:NS])
+        where.append((v_last, 0))
+
+        r0 = const.tile([1, NS], F32, name="r0")
+        v0 = where[0][0]
+        nc.gpsimd.tensor_tensor(out=r0[:], in0=v0[0:1, 0, 0:NS], in1=x0_sb[:], op=SUB)
+        nc.sync.dma_start(out=out[0:NS].rearrange("(o n) -> o n", o=1), in_=r0[:])
+
+        out_rows = out[NS : (STEPS + 1) * NS].rearrange("(p j i) -> p j i", p=P, j=J)
+
+        def transpose_pair(srcs, dst_f32):
+            xt = xt_ps.tile([P, 4, P], F32, name="xt")
+            n = len(srcs)
+            for t, s in enumerate(srcs):
+                for u in range(2):
+                    nc.tensor.transpose(xt[:, 2 * t + u, :], s[:, u : 2 * P : 2], ident[:])
+            nc.scalar.copy(
+                out=dst_f32,
+                in_=xt[:, 0 : 2 * n, :].rearrange("q (t u) c -> q t c u", u=2),
+            )
+
+        ab_f = ab_sb[:].bitcast(F32)
+        ab_g = const.tile([P, NS * 4], BF16, name="ab_g", align_bytes=64)
+        ab_gf = ab_g[:].bitcast(F32).rearrange("q (t c u) -> q t c u", t=3, u=2)
+        ab_codes = const.tile([P, NS], U32, name="ab_codes", align_bytes=64)
+        ab_scales = const.tile([P, NS], U8, name="ab_scales", align_bytes=64)
+        transpose_pair([ab_f[:, 0, :], ab_f[:, 1, :]], ab_gf[:, 0:2, :, :])
+        transpose_pair([ab_f[:, 2, :]], ab_gf[:, 2:3, :, :])
+        nc.vector.quantize_mx(
+            out=ab_codes[:, 0:256].bitcast(FP8X4), scales=ab_scales[:, 0:256], in_=ab_g[:, 0:1024]
+        )
+        nc.vector.quantize_mx(
+            out=ab_codes[:, 256:384].bitcast(FP8X4), scales=ab_scales[:, 256:384], in_=ab_g[:, 1024:1536]
+        )
+
+        grouped = {}
+        quant = {}
+        prods = {}
+
+        def stage_t(g):
+            gr = gpool.tile([P, GROUP * 4 * P], BF16, name="gr", align_bytes=64)
+            grf = gr[:].bitcast(F32).rearrange("q (t c u) -> q t c u", t=GROUP, u=2)
+            for h in range(GROUP // 2):
+                srcs = []
+                for t in range(2):
+                    vt, i = where[g * GROUP + 2 * h + t]
+                    srcs.append(vt[:].bitcast(F32)[:, i, :])
+                transpose_pair(srcs, grf[:, 2 * h : 2 * h + 2, :, :])
+            grouped[g] = gr
+
+        def stage_q(g):
+            codes = qpool.tile([P, GROUP * P], U32, name="codes", align_bytes=64)
+            scales = qpool.tile([P, GROUP * P], U8, name="scales", align_bytes=64)
+            nc.vector.quantize_mx(out=codes[:].bitcast(FP8X4), scales=scales[:], in_=grouped[g][:])
+            quant[g] = (codes, scales)
+
+        def stage_m(g):
+            codes, scales = quant[g]
+            prods[g] = []
+            for t in range(GROUP):
+                pr = pr_ps.tile([P, 512], F32, name="pr")
+                cols = slice(t * P, (t + 1) * P)
+                for lo, hi in ((0, 256), (256, 384)):
+                    nc.tensor.matmul_mx(
+                        out=pr[:, lo:hi],
+                        lhsT=codes[:, cols].bitcast(FP8X4),
+                        lhsT_scale=scales[:, cols],
+                        rhs=ab_codes[:, lo:hi].bitcast(FP8X4),
+                        rhs_scale=ab_scales[:, lo:hi],
+                        start=True,
+                        stop=True,
+                    )
+                prods[g].append(pr)
+
+        o_where = []
+        j0 = 0
+        for c, n in enumerate(STORE_CHUNKS):
+            ot = opool.tile([P, n, NS], F32, name="o%d" % c)
+            for i in range(n):
+                o_where.append((ot, i, j0, n))
+            j0 += n
+        assert j0 == J
+
+        def stage_c(g):
+            j = g * GROUP + OFFLOAD
+            ot, i, c0, n = o_where[j]
+            nc.scalar.copy(out=ot[:, i, :], in_=prods[g][OFFLOAD][:, 0:NS])
+
+        def stage_s(g):
+            for t in [OFFLOAD] + [t for t in range(GROUP) if t != OFFLOAD]:
+                j = g * GROUP + t
+                ot, i, c0, n = o_where[j]
+                vt, vi = where[j + 1]
+                if t == OFFLOAD:
+                    nc.gpsimd.tensor_tensor(out=ot[:, i, :], in0=ot[:, i, :], in1=vt[:, vi, 0:NS], op=SUB)
+                else:
+                    nc.vector.tensor_tensor(out=ot[:, i, :], in0=prods[g][t][:, 0:NS], in1=vt[:, vi, 0:NS], op=SUB)
+            for t in range(GROUP):
+                j = g * GROUP + t
+                ot, i, c0, n = o_where[j]
+                if i == n - 1:
+                    nc.sync.dma_start(out=out_rows[:, c0 : c0 + n, :], in_=ot[:])
+
+        stage_t(0)
+        stage_q(0)
+        stage_t(1)
+        for g in range(n_groups):
+            stage_m(g)
+            stage_c(g)
+            if g + 1 < n_groups:
+                stage_q(g + 1)
+            if g + 2 < n_groups:
+                stage_t(g + 2)
+            stage_s(g)

@@ -16,8 +16,8 @@ NA = 512
 STEPS = 8192
 J = STEPS // P
 GROUP = 4
-LOAD_CHUNKS = [4, 4, 8, 16, 32]
-STORE_CHUNKS = [8, 8, 8, 8, 8, 8, 8, 4, 2, 2]
+LOAD_CHUNKS = [4, 4, 8, 16, 33]
+STORE_CHUNKS = [16, 16, 8, 8, 8, 8]
 OFFLOAD = 0
 FLOPS = 2 * STEPS * NS * NA
 
@@ -46,19 +46,20 @@ def tile_constrainnet_t_kernel(tc, A, B, x0, net_input, T, out):
         nc.sync.dma_start(out=ab_sb[:, :, 0:NS], in_=A.rearrange("(r p) k -> p r k", p=P))
         nc.sync.dma_start(out=ab_sb[:, :, NS:NA], in_=B.rearrange("(r p) k -> p r k", p=P))
         v_rows = net_input[0 : STEPS * NA].rearrange("(p j k) -> p j k", p=P, j=J)
+        v_next = net_input[NA : (STEPS + 1) * NA].rearrange("(p j k) -> p j k", p=P, j=J)
         where = []
         j0 = 0
         for c, n in enumerate(LOAD_CHUNKS):
             vt = vpool.tile([P, n, NA], BF16, name="v%d" % c)
-            nc.sync.dma_start(out=vt[:], in_=v_rows[:, j0 : j0 + n, :])
+            if j0 + n <= J:
+                src = v_rows[:, j0 : j0 + n, :]
+            else:
+                src = v_next[:, j0 - 1 : j0 - 1 + n, :]
+            nc.sync.dma_start(out=vt[:], in_=src)
             for i in range(n):
                 where.append((vt, i))
             j0 += n
-        assert j0 == J
-        v_next = net_input[NA : (STEPS + 1) * NA].rearrange("(p j k) -> p j k", p=P, j=J)
-        v_last = vpool.tile([P, 1, NS], BF16, name="v_last")
-        nc.sync.dma_start(out=v_last[:], in_=v_next[:, J - 1 : J, 0:NS])
-        where.append((v_last, 0))
+        assert j0 == J + 1
 
         r0 = const.tile([1, NS], F32, name="r0")
         v0 = where[0][0]

@@ -17,7 +17,7 @@ STEPS = 8192
 J = STEPS // P
 GROUP = 4
 LOAD_CHUNKS = [4, 4, 8, 16, 33]
-STORE_CHUNKS = [16, 16, 8, 8, 8, 8]
+STORE_CHUNKS = [8, 8, 8, 8, 8, 4, 4, 4, 4, 4, 2, 2]
 OFFLOAD = 0
 FLOPS = 2 * STEPS * NS * NA
 

@@ -15,17 +15,20 @@ NS = 384
 NA = 512
 STEPS = 8192
 J = STEPS // P
-GROUP = 4
-LOAD_CHUNKS = [4, 4, 8, 16, 33]
+GROUPS = [2, 2] + [4] * 14 + [2, 2]
+LOAD_CHUNKS = [2, 2, 4, 8, 16, 33]
 STORE_CHUNKS = [8, 8, 8, 8, 8, 4, 4, 4, 4, 4, 2, 2]
-OFFLOAD = 0
+ROW0_AFTER = 8
+WARM_N = 512
 FLOPS = 2 * STEPS * NS * NA
 
 
 def tile_constrainnet_t_kernel(tc, A, B, x0, net_input, T, out):
     nc = tc.nc
     assert T == STEPS + 1
-    n_groups = J // GROUP
+    assert sum(GROUPS) == J and sum(STORE_CHUNKS) == J and sum(LOAD_CHUNKS) == J + 1
+    n_groups = len(GROUPS)
+    first = [sum(GROUPS[:g]) for g in range(n_groups)]
     with ExitStack() as ctx:
         const = ctx.enter_context(tc.tile_pool(name="const", bufs=1))
         vpool = ctx.enter_context(tc.tile_pool(name="vpool", bufs=1))
@@ -40,8 +43,16 @@ def tile_constrainnet_t_kernel(tc, A, B, x0, net_input, T, out):
         ident = const.tile([P, P], F32, name="ident")
         make_identity(nc, ident[:])
 
-        x0_sb = const.tile([1, NS], BF16, name="x0_sb")
-        nc.sync.dma_start(out=x0_sb[:], in_=x0.rearrange("(o n) -> o n", o=1))
+        warm_sb = const.tile([P, WARM_N], BF16, name="warm_sb")
+        nc.vector.memset(warm_sb[:], 0.0)
+
+        def warm(times):
+            dummy = pr_ps.tile([P, 512], F32, name="pr")
+            for i in range(times):
+                nc.tensor.matmul(dummy[:, 0:WARM_N], lhsT=warm_sb[:, 0:P], rhs=warm_sb[:], start=True, stop=True)
+
+        warm(6)
+
         ab_sb = const.tile([P, 3, NA], BF16, name="ab_sb")
         nc.sync.dma_start(out=ab_sb[:, :, 0:NS], in_=A.rearrange("(r p) k -> p r k", p=P))
         nc.sync.dma_start(out=ab_sb[:, :, NS:NA], in_=B.rearrange("(r p) k -> p r k", p=P))
@@ -59,22 +70,24 @@ def tile_constrainnet_t_kernel(tc, A, B, x0, net_input, T, out):
             for i in range(n):
                 where.append((vt, i))
             j0 += n
-        assert j0 == J + 1
+        x0_sb = const.tile([1, NS], BF16, name="x0_sb")
+        nc.sync.dma_start(out=x0_sb[:], in_=x0.rearrange("(o n) -> o n", o=1))
 
-        r0 = const.tile([1, NS], F32, name="r0")
-        v0 = where[0][0]
-        nc.gpsimd.tensor_tensor(out=r0[:], in0=v0[0:1, 0, 0:NS], in1=x0_sb[:], op=SUB)
-        nc.sync.dma_start(out=out[0:NS].rearrange("(o n) -> o n", o=1), in_=r0[:])
+        def row0():
+            r0 = const.tile([1, NS], F32, name="r0")
+            v0 = where[0][0]
+            nc.gpsimd.tensor_tensor(out=r0[:], in0=v0[0:1, 0, 0:NS], in1=x0_sb[:], op=SUB)
+            nc.sync.dma_start(out=out[0:NS].rearrange("(o n) -> o n", o=1), in_=r0[:])
 
         out_rows = out[NS : (STEPS + 1) * NS].rearrange("(p j i) -> p j i", p=P, j=J)
 
-        def transpose_pair(srcs, dst_f32):
+        def transpose_pair(srcs, dst_f32, copy):
             xt = xt_ps.tile([P, 4, P], F32, name="xt")
             n = len(srcs)
             for t, s in enumerate(srcs):
                 for u in range(2):
                     nc.tensor.transpose(xt[:, 2 * t + u, :], s[:, u : 2 * P : 2], ident[:])
-            nc.scalar.copy(
+            copy(
                 out=dst_f32,
                 in_=xt[:, 0 : 2 * n, :].rearrange("q (t u) c -> q t c u", u=2),
             )
@@ -84,8 +97,9 @@ def tile_constrainnet_t_kernel(tc, A, B, x0, net_input, T, out):
         ab_gf = ab_g[:].bitcast(F32).rearrange("q (t c u) -> q t c u", t=3, u=2)
         ab_codes = const.tile([P, NS], U32, name="ab_codes", align_bytes=64)
         ab_scales = const.tile([P, NS], U8, name="ab_scales", align_bytes=64)
-        transpose_pair([ab_f[:, 0, :], ab_f[:, 1, :]], ab_gf[:, 0:2, :, :])
-        transpose_pair([ab_f[:, 2, :]], ab_gf[:, 2:3, :, :])
+        transpose_pair([ab_f[:, 0, :], ab_f[:, 1, :]], ab_gf[:, 0:2, :, :], nc.vector.tensor_copy)
+        transpose_pair([ab_f[:, 2, :]], ab_gf[:, 2:3, :, :], nc.vector.tensor_copy)
+        warm(1)
         nc.vector.quantize_mx(
             out=ab_codes[:, 0:256].bitcast(FP8X4), scales=ab_scales[:, 0:256], in_=ab_g[:, 0:1024]
         )
@@ -98,26 +112,28 @@ def tile_constrainnet_t_kernel(tc, A, B, x0, net_input, T, out):
         prods = {}
 
         def stage_t(g):
-            gr = gpool.tile([P, GROUP * 4 * P], BF16, name="gr", align_bytes=64)
-            grf = gr[:].bitcast(F32).rearrange("q (t c u) -> q t c u", t=GROUP, u=2)
-            for h in range(GROUP // 2):
+            n = GROUPS[g]
+            gr = gpool.tile([P, n * 4 * P], BF16, name="gr", align_bytes=64)
+            grf = gr[:].bitcast(F32).rearrange("q (t c u) -> q t c u", t=n, u=2)
+            for h in range(n // 2):
                 srcs = []
                 for t in range(2):
-                    vt, i = where[g * GROUP + 2 * h + t]
+                    vt, i = where[first[g] + 2 * h + t]
                     srcs.append(vt[:].bitcast(F32)[:, i, :])
-                transpose_pair(srcs, grf[:, 2 * h : 2 * h + 2, :, :])
+                transpose_pair(srcs, grf[:, 2 * h : 2 * h + 2, :, :], nc.scalar.copy)
             grouped[g] = gr
 
         def stage_q(g):
-            codes = qpool.tile([P, GROUP * P], U32, name="codes", align_bytes=64)
-            scales = qpool.tile([P, GROUP * P], U8, name="scales", align_bytes=64)
+            n = GROUPS[g]
+            codes = qpool.tile([P, n * P], U32, name="codes", align_bytes=64)
+            scales = qpool.tile([P, n * P], U8, name="scales", align_bytes=64)
             nc.vector.quantize_mx(out=codes[:].bitcast(FP8X4), scales=scales[:], in_=grouped[g][:])
             quant[g] = (codes, scales)
 
         def stage_m(g):
             codes, scales = quant[g]
             prods[g] = []
-            for t in range(GROUP):
+            for t in range(GROUPS[g]):
                 pr = pr_ps.tile([P, 512], F32, name="pr")
                 cols = slice(t * P, (t + 1) * P)
                 for lo, hi in ((0, 256), (256, 384)):
@@ -139,31 +155,34 @@ def tile_constrainnet_t_kernel(tc, A, B, x0, net_input, T, out):
             for i in range(n):
                 o_where.append((ot, i, j0, n))
             j0 += n
-        assert j0 == J
+
+        def offloaded(g):
+            return 1 if GROUPS[g] == 4 else 0
 
         def stage_c(g):
-            j = g * GROUP + OFFLOAD
-            ot, i, c0, n = o_where[j]
-            nc.scalar.copy(out=ot[:, i, :], in_=prods[g][OFFLOAD][:, 0:NS])
+            for t in range(offloaded(g)):
+                ot, i, c0, n = o_where[first[g] + t]
+                nc.scalar.copy(out=ot[:, i, :], in_=prods[g][t][:, 0:NS])
 
         def stage_s(g):
-            for t in [OFFLOAD] + [t for t in range(GROUP) if t != OFFLOAD]:
-                j = g * GROUP + t
+            for t in range(GROUPS[g]):
+                j = first[g] + t
                 ot, i, c0, n = o_where[j]
                 vt, vi = where[j + 1]
-                if t == OFFLOAD:
+                if t < offloaded(g):
                     nc.gpsimd.tensor_tensor(out=ot[:, i, :], in0=ot[:, i, :], in1=vt[:, vi, 0:NS], op=SUB)
                 else:
                     nc.vector.tensor_tensor(out=ot[:, i, :], in0=prods[g][t][:, 0:NS], in1=vt[:, vi, 0:NS], op=SUB)
-            for t in range(GROUP):
-                j = g * GROUP + t
-                ot, i, c0, n = o_where[j]
+            for t in range(GROUPS[g]):
+                ot, i, c0, n = o_where[first[g] + t]
                 if i == n - 1:
                     nc.sync.dma_start(out=out_rows[:, c0 : c0 + n, :], in_=ot[:])
 
         stage_t(0)
         stage_q(0)
+        warm(2)
         stage_t(1)
+        warm(1)
         for g in range(n_groups):
             stage_m(g)
             stage_c(g)
@@ -172,3 +191,5 @@ def tile_constrainnet_t_kernel(tc, A, B, x0, net_input, T, out):
             if g + 2 < n_groups:
                 stage_t(g + 2)
             stage_s(g)
+            if g == ROW0_AFTER:
+                row0()

@@ -6,19 +6,22 @@ from concourse.masks import make_identity
 F32 = mybir.dt.float32
 BF16 = mybir.dt.bfloat16
 U32 = mybir.dt.uint32
+I32 = mybir.dt.int32
 U8 = mybir.dt.uint8
 FP8X4 = mybir.dt.float8_e4m3fn_x4
 SUB = mybir.AluOpType.subtract
 
 P = 128
 NS = 384
-NA = 512
+NI = 128
+NA = NS + NI
+R = NS // P
 STEPS = 8192
 J = STEPS // P
 GROUPS = [2, 2] + [4] * 14 + [2, 2]
-LOAD_CHUNKS = [2, 2, 4, 8, 16, 33]
-STORE_CHUNKS = [8, 8, 8, 8, 8, 4, 4, 4, 4, 4, 2, 2]
-ROW0_AFTER = 8
+LOAD_CHUNKS = [2, 2, 12, 16, 32]
+STORE_CHUNKS = [8] * 5 + [4] * 5 + [2, 2]
+EDGES_AFTER = 8
 WARM_N = 512
 FLOPS = 2 * STEPS * NS * NA
 
@@ -26,7 +29,7 @@ FLOPS = 2 * STEPS * NS * NA
 def tile_constrainnet_t_kernel(tc, A, B, x0, net_input, T, out):
     nc = tc.nc
     assert T == STEPS + 1
-    assert sum(GROUPS) == J and sum(STORE_CHUNKS) == J and sum(LOAD_CHUNKS) == J + 1
+    assert sum(GROUPS) == J and sum(STORE_CHUNKS) == J and sum(LOAD_CHUNKS) == J
     n_groups = len(GROUPS)
     first = [sum(GROUPS[:g]) for g in range(n_groups)]
     with ExitStack() as ctx:
@@ -42,6 +45,9 @@ def tile_constrainnet_t_kernel(tc, A, B, x0, net_input, T, out):
 
         ident = const.tile([P, P], F32, name="ident")
         make_identity(nc, ident[:])
+        shift = const.tile([P, P + 1], BF16, name="shift")
+        nc.gpsimd.memset(shift[:], 0.0)
+        make_identity(nc, shift[:, 0:P], nomemset=True)
 
         warm_sb = const.tile([P, WARM_N], BF16, name="warm_sb")
         nc.vector.memset(warm_sb[:], 0.0)
@@ -53,25 +59,30 @@ def tile_constrainnet_t_kernel(tc, A, B, x0, net_input, T, out):
 
         warm(6)
 
-        ab_sb = const.tile([P, 3, NA], BF16, name="ab_sb")
-        nc.sync.dma_start(out=ab_sb[:, :, 0:NS], in_=A.rearrange("(r p) k -> p r k", p=P))
-        nc.sync.dma_start(out=ab_sb[:, :, NS:NA], in_=B.rearrange("(r p) k -> p r k", p=P))
+        a_sb = const.tile([P, R * NS], BF16, name="a_sb")
+        b_sb = const.tile([P, R * NI], BF16, name="b_sb")
+        nc.sync.dma_start(out=a_sb[:], in_=A.rearrange("(p r) k -> p (r k)", p=P))
+        nc.sync.dma_start(out=b_sb[:], in_=B.rearrange("(p r) k -> p (r k)", p=P))
         v_rows = net_input[0 : STEPS * NA].rearrange("(p j k) -> p j k", p=P, j=J)
-        v_next = net_input[NA : (STEPS + 1) * NA].rearrange("(p j k) -> p j k", p=P, j=J)
         where = []
         j0 = 0
         for c, n in enumerate(LOAD_CHUNKS):
             vt = vpool.tile([P, n, NA], BF16, name="v%d" % c)
-            if j0 + n <= J:
-                src = v_rows[:, j0 : j0 + n, :]
-            else:
-                src = v_next[:, j0 - 1 : j0 - 1 + n, :]
-            nc.sync.dma_start(out=vt[:], in_=src)
+            nc.sync.dma_start(out=vt[:], in_=v_rows[:, j0 : j0 + n, :])
             for i in range(n):
                 where.append((vt, i))
             j0 += n
+        v_after = vpool.tile([P, 1, NS], BF16, name="v_after")
+        where.append((v_after, 0))
+        last = net_input[STEPS * NA : STEPS * NA + NS].rearrange("(o n) -> o n", o=1)
+        nc.sync.dma_start(out=v_after[P - 1 : P, 0, :], in_=last)
         x0_sb = const.tile([1, NS], BF16, name="x0_sb")
         nc.sync.dma_start(out=x0_sb[:], in_=x0.rearrange("(o n) -> o n", o=1))
+
+        def rows_after():
+            pr = pr_ps.tile([P, 512], F32, name="pr")
+            nc.tensor.matmul(pr[:, 0:NS], lhsT=shift[:, 1 : P + 1], rhs=where[0][0][:, 0, 0:NS], start=True, stop=True)
+            nc.scalar.copy(out=v_after[0 : P - 1, 0, :], in_=pr[0 : P - 1, 0:NS])
 
         def row0():
             r0 = const.tile([1, NS], F32, name="r0")
@@ -92,19 +103,33 @@ def tile_constrainnet_t_kernel(tc, A, B, x0, net_input, T, out):
                 in_=xt[:, 0 : 2 * n, :].rearrange("q (t u) c -> q t c u", u=2),
             )
 
+        ab_sb = const.tile([P, R, NA], BF16, name="ab_sb")
+        nc.vector.tensor_copy(out=ab_sb[:, :, 0:NS], in_=a_sb[:].rearrange("p (r k) -> p r k", r=R))
+        nc.scalar.copy(out=ab_sb[:, :, NS:NA], in_=b_sb[:].rearrange("p (r k) -> p r k", r=R))
         ab_f = ab_sb[:].bitcast(F32)
         ab_g = const.tile([P, NS * 4], BF16, name="ab_g", align_bytes=64)
         ab_gf = ab_g[:].bitcast(F32).rearrange("q (t c u) -> q t c u", t=3, u=2)
-        ab_codes = const.tile([P, NS], U32, name="ab_codes", align_bytes=64)
-        ab_scales = const.tile([P, NS], U8, name="ab_scales", align_bytes=64)
+        rp_codes = const.tile([P, NS], U32, name="rp_codes", align_bytes=64)
+        rp_scales = const.tile([P, NS], U8, name="rp_scales", align_bytes=64)
+        nc.gpsimd.memset(rp_scales[:], 0)
         transpose_pair([ab_f[:, 0, :], ab_f[:, 1, :]], ab_gf[:, 0:2, :, :], nc.vector.tensor_copy)
         transpose_pair([ab_f[:, 2, :]], ab_gf[:, 2:3, :, :], nc.vector.tensor_copy)
         warm(1)
         nc.vector.quantize_mx(
-            out=ab_codes[:, 0:256].bitcast(FP8X4), scales=ab_scales[:, 0:256], in_=ab_g[:, 0:1024]
+            out=rp_codes[:, 0:256].bitcast(FP8X4), scales=rp_scales[:, 0:256], in_=ab_g[:, 0:1024]
         )
         nc.vector.quantize_mx(
-            out=ab_codes[:, 256:384].bitcast(FP8X4), scales=ab_scales[:, 256:384], in_=ab_g[:, 1024:1536]
+            out=rp_codes[:, 256:384].bitcast(FP8X4), scales=rp_scales[:, 256:384], in_=ab_g[:, 1024:1536]
+        )
+        ab_codes = const.tile([P, NS], U32, name="ab_codes", align_bytes=64)
+        ab_scales = const.tile([P, NS], U8, name="ab_scales", align_bytes=64)
+        nc.vector.tensor_copy(
+            out=ab_codes[:].bitcast(I32).rearrange("q (p r) -> q p r", r=R),
+            in_=rp_codes[:].bitcast(I32).rearrange("q (r p) -> q p r", r=R),
+        )
+        nc.gpsimd.tensor_copy(
+            out=ab_scales[:].rearrange("q (p r) -> q r p", r=R),
+            in_=rp_scales[:].rearrange("q (r p) -> q r p", r=R),
         )
 
         grouped = {}
@@ -191,5 +216,6 @@ def tile_constrainnet_t_kernel(tc, A, B, x0, net_input, T, out):
             if g + 2 < n_groups:
                 stage_t(g + 2)
             stage_s(g)
-            if g == ROW0_AFTER:
+            if g == EDGES_AFTER:
+                rows_after()
                 row0()

@@ -20,7 +20,7 @@ STEPS = 8192
 J = STEPS // P
 GROUPS = [2, 2] + [4] * 14 + [2, 2]
 LOAD_CHUNKS = [2, 2, 12, 16, 32]
-STORE_CHUNKS = [8] * 5 + [4] * 5 + [2, 2]
+STORE_CHUNKS = [8] * 7 + [4, 2, 2]
 EDGES_AFTER = 8
 WARM_N = 512
 FLOPS = 2 * STEPS * NS * NA
@@ -57,7 +57,7 @@ def tile_constrainnet_t_kernel(tc, A, B, x0, net_input, T, out):
             for i in range(times):
                 nc.tensor.matmul(dummy[:, 0:WARM_N], lhsT=warm_sb[:, 0:P], rhs=warm_sb[:], start=True, stop=True)
 
-        warm(6)
+        warm(5)
 
         a_sb = const.tile([P, R * NS], BF16, name="a_sb")
         b_sb = const.tile([P, R * NI], BF16, name="b_sb")
@@ -152,7 +152,13 @@ def tile_constrainnet_t_kernel(tc, A, B, x0, net_input, T, out):
             n = GROUPS[g]
             codes = qpool.tile([P, n * P], U32, name="codes", align_bytes=64)
             scales = qpool.tile([P, n * P], U8, name="scales", align_bytes=64)
-            nc.vector.quantize_mx(out=codes[:].bitcast(FP8X4), scales=scales[:], in_=grouped[g][:])
+            for h in range(n // 2):
+                cols = slice(2 * h * P, 2 * (h + 1) * P)
+                nc.vector.quantize_mx(
+                    out=codes[:, cols].bitcast(FP8X4),
+                    scales=scales[:, cols],
+                    in_=grouped[g][:, 8 * h * P : 8 * (h + 1) * P],
+                )
             quant[g] = (codes, scales)
 
         def stage_m(g):

@@ -19,8 +19,8 @@ R = NS // P
 STEPS = 8192
 J = STEPS // P
 GROUPS = [2, 2] + [4] * 14 + [2, 2]
-LOAD_CHUNKS = [2, 2, 12, 16, 32]
-STORE_CHUNKS = [8] * 7 + [4, 2, 2]
+LOAD_CHUNKS = [4, 12, 16, 32]
+STORE_CHUNKS = [16] + [8] * 5 + [4, 2, 2]
 EDGES_AFTER = 8
 WARM_N = 512
 FLOPS = 2 * STEPS * NS * NA

from contextlib import ExitStack

import concourse.mybir as mybir
from concourse.masks import make_identity

F32 = mybir.dt.float32
BF16 = mybir.dt.bfloat16
U32 = mybir.dt.uint32
I32 = mybir.dt.int32
U8 = mybir.dt.uint8
FP8X4 = mybir.dt.float8_e4m3fn_x4
SUB = mybir.AluOpType.subtract

P = 128
NS = 384
NI = 128
NA = NS + NI
R = NS // P
STEPS = 8192
J = STEPS // P
GROUPS = [2, 2] + [4] * 14 + [2, 2]
LOAD_CHUNKS = [4, 12, 16, 32]
STORE_CHUNKS = [16] + [8] * 5 + [4, 2, 2]
EDGES_AFTER = 8
WARM_N = 512
FLOPS = 2 * STEPS * NS * NA


def tile_constrainnet_t_kernel(tc, A, B, x0, net_input, T, out):
    nc = tc.nc
    assert T == STEPS + 1
    assert sum(GROUPS) == J and sum(STORE_CHUNKS) == J and sum(LOAD_CHUNKS) == J
    n_groups = len(GROUPS)
    first = [sum(GROUPS[:g]) for g in range(n_groups)]
    with ExitStack() as ctx:
        const = ctx.enter_context(tc.tile_pool(name="const", bufs=1))
        vpool = ctx.enter_context(tc.tile_pool(name="vpool", bufs=1))
        opool = ctx.enter_context(tc.tile_pool(name="opool", bufs=1))
        gpool = ctx.enter_context(tc.tile_pool(name="gpool", bufs=3))
        qpool = ctx.enter_context(tc.tile_pool(name="qpool", bufs=3))
        xt_ps = ctx.enter_context(tc.psum_pool(name="xt_ps", bufs=3))
        pr_ps = ctx.enter_context(tc.psum_pool(name="pr_ps", bufs=5))

        ctx.enter_context(tc.manual_schedule())

        ident = const.tile([P, P], F32, name="ident")
        make_identity(nc, ident[:])
        shift = const.tile([P, P + 1], BF16, name="shift")
        nc.gpsimd.memset(shift[:], 0.0)
        make_identity(nc, shift[:, 0:P], nomemset=True)

        warm_sb = const.tile([P, WARM_N], BF16, name="warm_sb")
        nc.vector.memset(warm_sb[:], 0.0)

        def warm(times):
            dummy = pr_ps.tile([P, 512], F32, name="pr")
            for i in range(times):
                nc.tensor.matmul(dummy[:, 0:WARM_N], lhsT=warm_sb[:, 0:P], rhs=warm_sb[:], start=True, stop=True)

        warm(5)

        a_sb = const.tile([P, R * NS], BF16, name="a_sb")
        b_sb = const.tile([P, R * NI], BF16, name="b_sb")
        nc.sync.dma_start(out=a_sb[:], in_=A.rearrange("(p r) k -> p (r k)", p=P))
        nc.sync.dma_start(out=b_sb[:], in_=B.rearrange("(p r) k -> p (r k)", p=P))
        v_rows = net_input[0 : STEPS * NA].rearrange("(p j k) -> p j k", p=P, j=J)
        where = []
        j0 = 0
        for c, n in enumerate(LOAD_CHUNKS):
            vt = vpool.tile([P, n, NA], BF16, name="v%d" % c)
            nc.sync.dma_start(out=vt[:], in_=v_rows[:, j0 : j0 + n, :])
            for i in range(n):
                where.append((vt, i))
            j0 += n
        v_after = vpool.tile([P, 1, NS], BF16, name="v_after")
        where.append((v_after, 0))
        last = net_input[STEPS * NA : STEPS * NA + NS].rearrange("(o n) -> o n", o=1)
        nc.sync.dma_start(out=v_after[P - 1 : P, 0, :], in_=last)
        x0_sb = const.tile([1, NS], BF16, name="x0_sb")
        nc.sync.dma_start(out=x0_sb[:], in_=x0.rearrange("(o n) -> o n", o=1))

        def rows_after():
            pr = pr_ps.tile([P, 512], F32, name="pr")
            nc.tensor.matmul(pr[:, 0:NS], lhsT=shift[:, 1 : P + 1], rhs=where[0][0][:, 0, 0:NS], start=True, stop=True)
            nc.scalar.copy(out=v_after[0 : P - 1, 0, :], in_=pr[0 : P - 1, 0:NS])

        def row0():
            r0 = const.tile([1, NS], F32, name="r0")
            v0 = where[0][0]
            nc.gpsimd.tensor_tensor(out=r0[:], in0=v0[0:1, 0, 0:NS], in1=x0_sb[:], op=SUB)
            nc.sync.dma_start(out=out[0:NS].rearrange("(o n) -> o n", o=1), in_=r0[:])

        out_rows = out[NS : (STEPS + 1) * NS].rearrange("(p j i) -> p j i", p=P, j=J)

        def transpose_pair(srcs, dst_f32, copy):
            xt = xt_ps.tile([P, 4, P], F32, name="xt")
            n = len(srcs)
            for t, s in enumerate(srcs):
                for u in range(2):
                    nc.tensor.transpose(xt[:, 2 * t + u, :], s[:, u : 2 * P : 2], ident[:])
            copy(
                out=dst_f32,
                in_=xt[:, 0 : 2 * n, :].rearrange("q (t u) c -> q t c u", u=2),
            )

        ab_sb = const.tile([P, R, NA], BF16, name="ab_sb")
        nc.vector.tensor_copy(out=ab_sb[:, :, 0:NS], in_=a_sb[:].rearrange("p (r k) -> p r k", r=R))
        nc.scalar.copy(out=ab_sb[:, :, NS:NA], in_=b_sb[:].rearrange("p (r k) -> p r k", r=R))
        ab_f = ab_sb[:].bitcast(F32)
        ab_g = const.tile([P, NS * 4], BF16, name="ab_g", align_bytes=64)
        ab_gf = ab_g[:].bitcast(F32).rearrange("q (t c u) -> q t c u", t=3, u=2)
        rp_codes = const.tile([P, NS], U32, name="rp_codes", align_bytes=64)
        rp_scales = const.tile([P, NS], U8, name="rp_scales", align_bytes=64)
        nc.gpsimd.memset(rp_scales[:], 0)
        transpose_pair([ab_f[:, 0, :], ab_f[:, 1, :]], ab_gf[:, 0:2, :, :], nc.vector.tensor_copy)
        transpose_pair([ab_f[:, 2, :]], ab_gf[:, 2:3, :, :], nc.vector.tensor_copy)
        warm(1)
        nc.vector.quantize_mx(
            out=rp_codes[:, 0:256].bitcast(FP8X4), scales=rp_scales[:, 0:256], in_=ab_g[:, 0:1024]
        )
        nc.vector.quantize_mx(
            out=rp_codes[:, 256:384].bitcast(FP8X4), scales=rp_scales[:, 256:384], in_=ab_g[:, 1024:1536]
        )
        ab_codes = const.tile([P, NS], U32, name="ab_codes", align_bytes=64)
        ab_scales = const.tile([P, NS], U8, name="ab_scales", align_bytes=64)
        nc.vector.tensor_copy(
            out=ab_codes[:].bitcast(I32).rearrange("q (p r) -> q p r", r=R),
            in_=rp_codes[:].bitcast(I32).rearrange("q (r p) -> q p r", r=R),
        )
        nc.gpsimd.tensor_copy(
            out=ab_scales[:].rearrange("q (p r) -> q r p", r=R),
            in_=rp_scales[:].rearrange("q (r p) -> q r p", r=R),
        )

        grouped = {}
        quant = {}
        prods = {}

        def stage_t(g):
            n = GROUPS[g]
            gr = gpool.tile([P, n * 4 * P], BF16, name="gr", align_bytes=64)
            grf = gr[:].bitcast(F32).rearrange("q (t c u) -> q t c u", t=n, u=2)
            for h in range(n // 2):
                srcs = []
                for t in range(2):
                    vt, i = where[first[g] + 2 * h + t]
                    srcs.append(vt[:].bitcast(F32)[:, i, :])
                transpose_pair(srcs, grf[:, 2 * h : 2 * h + 2, :, :], nc.scalar.copy)
            grouped[g] = gr

        def stage_q(g):
            n = GROUPS[g]
            codes = qpool.tile([P, n * P], U32, name="codes", align_bytes=64)
            scales = qpool.tile([P, n * P], U8, name="scales", align_bytes=64)
            for h in range(n // 2):
                cols = slice(2 * h * P, 2 * (h + 1) * P)
                nc.vector.quantize_mx(
                    out=codes[:, cols].bitcast(FP8X4),
                    scales=scales[:, cols],
                    in_=grouped[g][:, 8 * h * P : 8 * (h + 1) * P],
                )
            quant[g] = (codes, scales)

        def stage_m(g):
            codes, scales = quant[g]
            prods[g] = []
            for t in range(GROUPS[g]):
                pr = pr_ps.tile([P, 512], F32, name="pr")
                cols = slice(t * P, (t + 1) * P)
                for lo, hi in ((0, 256), (256, 384)):
                    nc.tensor.matmul_mx(
                        out=pr[:, lo:hi],
                        lhsT=codes[:, cols].bitcast(FP8X4),
                        lhsT_scale=scales[:, cols],
                        rhs=ab_codes[:, lo:hi].bitcast(FP8X4),
                        rhs_scale=ab_scales[:, lo:hi],
                        start=True,
                        stop=True,
                    )
                prods[g].append(pr)

        o_where = []
        j0 = 0
        for c, n in enumerate(STORE_CHUNKS):
            ot = opool.tile([P, n, NS], F32, name="o%d" % c)
            for i in range(n):
                o_where.append((ot, i, j0, n))
            j0 += n

        def offloaded(g):
            return 1 if GROUPS[g] == 4 else 0

        def stage_c(g):
            for t in range(offloaded(g)):
                ot, i, c0, n = o_where[first[g] + t]
                nc.scalar.copy(out=ot[:, i, :], in_=prods[g][t][:, 0:NS])

        def stage_s(g):
            for t in range(GROUPS[g]):
                j = first[g] + t
                ot, i, c0, n = o_where[j]
                vt, vi = where[j + 1]
                if t < offloaded(g):
                    nc.gpsimd.tensor_tensor(out=ot[:, i, :], in0=ot[:, i, :], in1=vt[:, vi, 0:NS], op=SUB)
                else:
                    nc.vector.tensor_tensor(out=ot[:, i, :], in0=prods[g][t][:, 0:NS], in1=vt[:, vi, 0:NS], op=SUB)
            for t in range(GROUPS[g]):
                ot, i, c0, n = o_where[first[g] + t]
                if i == n - 1:
                    nc.sync.dma_start(out=out_rows[:, c0 : c0 + n, :], in_=ot[:])

        stage_t(0)
        stage_q(0)
        warm(2)
        stage_t(1)
        warm(1)
        for g in range(n_groups):
            stage_m(g)
            stage_c(g)
            if g + 1 < n_groups:
                stage_q(g + 1)
            if g + 2 < n_groups:
                stage_t(g + 2)
            stage_s(g)
            if g == EDGES_AFTER:
                rows_after()
                row0()
